import numpy as np
import ml_dtypes


def mxq(x, axis, fmt="e4m3"):
    dtype, down = {"e4m3": (ml_dtypes.float8_e4m3fn, 7), "e5m2": (ml_dtypes.float8_e5m2, 14)}[fmt]
    v = np.moveaxis(np.asarray(x, np.float32).astype(ml_dtypes.bfloat16).astype(np.float64), axis, -1)
    blocks = v.reshape(v.shape[:-1] + (-1, 32))
    amax = np.abs(blocks).max(-1, keepdims=True)
    byte = np.maximum(np.where(amax > 0, np.frexp(amax)[1] - 1 + 127, 0) - down, 1)
    scale = np.exp2(byte - 127.0)
    codes = (blocks / scale).astype(np.float32).astype(dtype).astype(np.float64)
    return np.moveaxis((codes * scale).reshape(v.shape), -1, axis)


WIDE = False


def mx_kscale(k):
    if not WIDE:
        return np.ones(k)
    levels = np.array([10, -10, 5, -5, 0])
    if k % 512:
        return np.exp2(np.random.permutation(np.resize(levels, k // 32))).repeat(32)
    a = np.empty((k // 512, 16))
    for p in range(k // 512):
        a[p, :8] = np.random.permutation(np.resize(levels, 8))
        for g in range(8):
            far = levels[np.abs(levels - a[p, g]) >= 10]
            a[p, g + 8] = far[np.random.randint(len(far))]
    return np.exp2(a.ravel()).repeat(32)


BF16 = ml_dtypes.bfloat16


def bf(x):
    return np.asarray(x, np.float32).astype(BF16)


def f64(x):
    return np.asarray(x).astype(np.float64)


B, S, H, I, G = 4, 1024, 512, 1024, 4
T = B * S


def grouped_linear(xf, w, b):
    g, dout, din = w.shape
    xg = xf.reshape(g, -1, din)
    y = (mxq(xg, 2, "e4m3") @ mxq(w, 2, "e4m3").transpose(0, 2, 1)) + b[:, None, :]
    return y.reshape(-1, dout)


def draw0():
    s, t = mx_kscale(H), mx_kscale(I)
    return {"hf": bf(np.random.standard_normal((T, H)) * s),
            "g1_w": bf(np.random.standard_normal((G, I, H)) / np.sqrt(H) / s[None, None, :] * t[None, :, None]),
            "g1_b": bf(np.random.standard_normal((G, I)) * 0.3 * t[None, :]),
            "g2_w": bf(np.random.standard_normal((G, H, I)) / np.sqrt(I) / t[None, None, :]),
            "g2_b": bf(np.random.standard_normal((G, H)) * 0.3)}


def core(hf, g1_w, g1_b, g2_w, g2_b):
    y = grouped_linear(f64(hf), f64(g1_w), f64(g1_b))
    return grouped_linear(y, f64(g2_w), f64(g2_b))


def e4m3fn_bytes(y):
    return np.clip(np.asarray(y, np.float64), -448.0, 448.0).astype(np.float32).astype(ml_dtypes.float8_e4m3fn).view(np.uint8)


def e4m3fn_values(b):
    return np.asarray(b, np.uint8).view(ml_dtypes.float8_e4m3fn).astype(np.float64)


def setup_inputs():
    d = draw0()
    x0 = np.asarray(d['hf']).astype(np.float64)
    s = (np.max(np.abs(x0), axis=(0,), keepdims=True) / 448.0).astype(np.float32)
    out = {}
    for k, v in d.items():
        if k == 'hf':
            out['hf_bytes'] = e4m3fn_bytes(x0 / s.astype(np.float64))
            out['hf_scale'] = s
        else:
            out[k] = v
    return out


def reference(hf_bytes, hf_scale, g1_w, g1_b, g2_w, g2_b):
    return core(e4m3fn_values(hf_bytes) * hf_scale.astype(np.float64), g1_w, g1_b, g2_w, g2_b)

@@ -1,0 +1,334 @@
+from contextlib import ExitStack
+
+import concourse.mybir as mybir
+from concourse.masks import make_identity
+
+F32 = mybir.dt.float32
+BF16 = mybir.dt.bfloat16
+U32 = mybir.dt.uint32
+U8 = mybir.dt.uint8
+FP8 = mybir.dt.float8_e4m3fn
+FP8X4 = mybir.dt.float8_e4m3fn_x4
+ADD = mybir.AluOpType.add
+MULT = mybir.AluOpType.mult
+IDENTITY = mybir.ActivationFunctionType.Identity
+
+FLOPS = 2 * 4096 * 512 * 1024 * 2
+
+P = 128
+G = 4
+SLOTS = 8
+
+
+def tile_dummytemodel_pa_t_kernel(tc, hf_bytes, hf_scale, g1_w, g1_b, g2_w, g2_b, out):
+    nc = tc.nc
+    with ExitStack() as ctx:
+        const = ctx.enter_context(tc.tile_pool(name="const", bufs=1))
+        raw = ctx.enter_context(tc.tile_pool(name="raw", bufs=1))
+        work = ctx.enter_context(tc.tile_pool(name="work", bufs=3))
+        codes_pool = ctx.enter_context(tc.tile_pool(name="codes", bufs=2))
+        psum = ctx.enter_context(tc.psum_pool(name="psum", bufs=1))
+
+        ident = const.tile([P, P], F32)
+        make_identity(nc, ident[:])
+        warm = const.tile([P, 1], F32)
+        warm_out = const.tile([P, 1], F32)
+        nc.gpsimd.memset(warm[:], 0.0)
+
+        hf_view = hf_bytes.rearrange("(g p r) k -> g p r k", g=G, r=8)
+        out_view = out.rearrange("(g p r) n -> g p r n", g=G, r=8)
+        scale = const.tile([P, 512], F32)
+        bias1_raw = const.tile([P, 8, 4], BF16)
+        bias1 = const.tile([P, 8, 4], F32)
+        bias2 = const.tile([P, G, 512], BF16)
+        hfb, w1raw, w2raw = [], [], []
+        for g in range(G):
+            hf_tile = raw.tile([P, 8, 512], U8, tag="hfb%d" % g)
+            hfb.append(hf_tile)
+            for h in range(2):
+                w1_tile = raw.tile([P, 4, 512], BF16, tag="w1_%d_%d" % (g, h))
+                w1raw.append(w1_tile)
+            w2_tile = raw.tile([P, 4, 1024], BF16, tag="w2_%d" % g)
+            w2raw.append(w2_tile)
+
+        def load_w1(g, h):
+            nc.sync.dma_start(
+                out=w1raw[2 * g + h][:],
+                in_=g1_w[g].rearrange("(h m t) k -> h m t k", h=2, t=4)[h],
+            )
+
+        def load_w2(g):
+            nc.sync.dma_start(out=w2raw[g][:], in_=g2_w[g].rearrange("(j p) k -> p j k", j=4))
+
+        nc.sync.dma_start(out=scale[:], in_=hf_scale.rearrange("o k -> (o k)").partition_broadcast(P))
+        nc.sync.dma_start(out=hfb[0][:, 0:4, :], in_=hf_view[0][:, 0:4, :])
+        load_w1(0, 0)
+        load_w1(0, 1)
+        nc.sync.dma_start(out=bias1_raw[:], in_=g1_b.rearrange("g (h m t) -> m (g h) t", h=2, t=4))
+        nc.sync.dma_start(out=hfb[0][:, 4:8, :], in_=hf_view[0][:, 4:8, :])
+        load_w2(0)
+        nc.sync.dma_start(
+            out=bias2[:].rearrange("p g n -> p (g n)"),
+            in_=g2_b.rearrange("g n -> (g n)").partition_broadcast(P),
+        )
+        for g in range(1, G):
+            nc.sync.dma_start(out=hfb[g][:], in_=hf_view[g])
+            load_w1(g, 0)
+            load_w1(g, 1)
+            load_w2(g)
+
+        scaled = {}
+
+        def scale_rows(i, r):
+            if i >= SLOTS:
+                return
+            if r == 0:
+                hb = work.tile([P, 4, 512], BF16, tag="hb")
+                scaled[i] = hb
+            nc.vector.tensor_tensor(
+                out=scaled[i][:, r, :],
+                in0=hfb[i // 2][:, 4 * (i % 2) + r, :].bitcast(FP8),
+                in1=scale[:],
+                op=MULT,
+            )
+
+        grouped = {}
+        xt = {}
+
+        def words(unit, row):
+            kind, a, b = unit
+            if kind == "hf":
+                return scaled[a][:, row, :].bitcast(F32)
+            if kind == "w1":
+                return w1raw[2 * a + b][:, row, :].bitcast(F32)
+            return w2raw[a][:, row, 512 * b : 512 * (b + 1)].bitcast(F32)
+
+        def turn(unit, j, bank):
+            x = psum.tile([P, 512], F32, tag=bank)
+            xt[unit, j] = x
+            view = x[:].rearrange("p (a u c) -> p a u c", a=2, u=2)
+            for a in range(2):
+                w = words(unit, 2 * j + a)
+                for u in range(2):
+                    nc.tensor.transpose(view[:, a, u, :], w[:, u:256:2], ident[:])
+
+        def gather(unit, j, engine):
+            if j == 0:
+                grp = work.tile([P, 2048], BF16, tag="grp", align_bytes=64)
+                grouped[unit] = grp
+            dst = grouped[unit][:].bitcast(F32)[:, 512 * j : 512 * (j + 1)].rearrange("p (a c u) -> p a c u", a=2, u=2)
+            srcv = xt[unit, j][:].rearrange("p (a u c) -> p a c u", a=2, u=2)
+            if engine == "s":
+                nc.scalar.copy(out=dst, in_=srcv)
+            else:
+                nc.vector.tensor_copy(out=dst, in_=srcv)
+
+        codes = {}
+
+        def quantize(unit, tag):
+            q = codes_pool.tile([P, 512], U32, tag=tag, align_bytes=64)
+            s = codes_pool.tile([P, 512], U8, tag=tag + "s", align_bytes=64)
+            codes[unit] = (q, s)
+            nc.vector.quantize_mx(out=q[:].bitcast(FP8X4), scales=s[:], in_=grouped[unit][:])
+
+        def prep_quantize(unit):
+            kind, a, b = unit
+            quantize(unit, "hfq" if kind == "hf" else "%sq%d" % (kind, b))
+
+        def mx(dst, left, lcols, right, rcols, start, stop):
+            lq, ls = codes[left]
+            rq, rs = codes[right]
+            nc.tensor.matmul_mx(
+                out=dst,
+                lhsT=lq[:, lcols].bitcast(FP8X4),
+                lhsT_scale=ls[:, lcols],
+                rhs=rq[:, rcols].bitcast(FP8X4),
+                rhs_scale=rs[:, rcols],
+                start=start,
+                stop=stop,
+            )
+
+        def mode(i, h):
+            if i == SLOTS - 1:
+                return "direct" if h == 0 else "pairs"
+            return "half" if i % 2 == 0 and h == 1 else "pairs"
+
+        first = {}
+        pairs = {}
+
+        def stage1(i, h):
+            m = mode(i, h)
+            for b in range(4):
+                bank = psum.tile([P, 512], F32, tag="c%d" % b)
+                first[i, h, b] = bank
+                if m == "pairs":
+                    mx(bank[:], ("w1", i // 2, h), slice(128 * b, 128 * (b + 1)), ("hf", i, 0), slice(0, 512), True, True)
+                elif m == "half" and b < 2:
+                    for e in range(2):
+                        t = 2 * b + e
+                        mx(bank[:, 256 * e : 256 * (e + 1)], ("w1", i // 2, h), slice(128 * t, 128 * (t + 1)), ("hf", i, 0), slice(0, 256), True, True)
+                else:
+                    for t in range(4):
+                        mx(bank[:, 128 * t : 128 * (t + 1)], ("w1", i // 2, h), slice(128 * t, 128 * (t + 1)), ("hf", i, 0), slice(128 * b, 128 * (b + 1)), True, True)
+
+        def bias_planes(i, h, ts):
+            m = mode(i, h)
+            if m == "direct":
+                return
+            n = 512 if m == "pairs" else 256
+            if ts[0] == 0:
+                y2 = work.tile([P, 2, 512, 2], BF16, tag="y2", align_bytes=64)
+                pairs[i, h] = y2
+            for t in ts:
+                src = first[i, h, t][:] if m == "pairs" else first[i, h, t // 2][:, 256 * (t % 2) : 256 * (t % 2 + 1)]
+                nc.scalar.activation(
+                    out=pairs[i, h][:, t // 2, 0:n, t % 2],
+                    in_=src,
+                    func=IDENTITY,
+                    bias=bias1[:, 2 * (i // 2) + h, t : t + 1],
+                )
+
+        def y_tile(i, h):
+            if ("y", i, h) not in grouped:
+                yg = work.tile([P, 2048], BF16, tag="yg", align_bytes=64)
+                grouped["y", i, h] = yg
+            return grouped["y", i, h]
+
+        def join_pairs(i, h):
+            m = mode(i, h)
+            yg = y_tile(i, h)
+            if m == "direct":
+                return
+            n = 512 if m == "pairs" else 256
+            nc.vector.tensor_copy(
+                out=yg[:].bitcast(F32)[:, 0 : 2 * n].rearrange("p (n u) -> p n u", u=2),
+                in_=pairs[i, h][:].rearrange("p u n e -> p (u n e)").bitcast(F32).rearrange("p (u n) -> p n u", u=2)[:, 0:n, :],
+            )
+
+        def direct(i, h):
+            m = mode(i, h)
+            if m == "pairs":
+                return
+            yg = y_tile(i, h)
+            for b in range(0 if m == "direct" else 2, 4):
+                nc.vector.tensor_tensor(
+                    out=yg[:, 512 * b : 512 * (b + 1)].rearrange("p (n t) -> p n t", t=4),
+                    in0=first[i, h, b][:].rearrange("p (t n) -> p n t", t=4),
+                    in1=bias1[:, 2 * (i // 2) + h : 2 * (i // 2) + h + 1, :].to_broadcast([P, 128, 4]),
+                    op=ADD,
+                )
+
+        second = {}
+        results = {}
+
+        def stage2(i, rs):
+            if i < 0:
+                return
+            for r in rs:
+                bank = psum.tile([P, 512], F32, tag="d%d" % (r % 2))
+                second[i, r] = bank
+                for h in range(2):
+                    mx(bank[:], ("y", i, h), slice(128 * r, 128 * (r + 1)), ("w2", i // 2, h), slice(0, 512), h == 0, h == 1)
+
+        def finish(i, rs):
+            if i < 0:
+                return
+            if rs[0] == 0:
+                o = work.tile([P, 4, 512], F32, tag="o")
+                results[i] = o
+            for r in rs:
+                nc.vector.tensor_tensor(out=results[i][:, r, :], in0=second[i, r][:], in1=bias2[:, i // 2, :], op=ADD)
+
+        def store(i, r0, n):
+            if i < 0:
+                return
+            first_row = 4 * (i % 2) + r0
+            nc.sync.dma_start(out=out_view[i // 2][:, first_row : first_row + n, :], in_=results[i][:, r0 : r0 + n, :])
+
+        def preps(i):
+            g = i // 2
+            if i == SLOTS - 1:
+                return []
+            if i % 2 == 0:
+                return [("hf", i + 1, 0), ("w2", g, 0), ("w2", g, 1)]
+            return [("w1", g + 1, 0), ("hf", i + 1, 0), ("w1", g + 1, 1)]
+
+        with tc.manual_schedule():
+            nc.scalar.activation(out=warm_out[:], in_=warm[:], func=IDENTITY)
+            h0, a0, a1 = ("hf", 0, 0), ("w1", 0, 0), ("w1", 0, 1)
+            scale_rows(0, 0)
+            scale_rows(0, 1)
+            turn(h0, 0, "x0")
+            gather(h0, 0, "s")
+            scale_rows(0, 2)
+            scale_rows(0, 3)
+            turn(a0, 0, "c0")
+            turn(h0, 1, "x1")
+            turn(a0, 1, "c1")
+            gather(a0, 0, "s")
+            gather(h0, 1, "s")
+            gather(a0, 1, "v")
+            nc.vector.tensor_copy(out=bias1[:], in_=bias1_raw[:])
+            prep_quantize(h0)
+            prep_quantize(a0)
+            turn(a1, 0, "c2")
+            turn(a1, 1, "c3")
+            gather(a1, 0, "s")
+            gather(a1, 1, "v")
+            scale_rows(1, 0)
+            prep_quantize(a1)
+            for r in range(1, 4):
+                scale_rows(1, r)
+
+            for i in range(SLOTS):
+                todo = preps(i)
+
+                def prep(k):
+                    if k < len(todo):
+                        for j in range(2):
+                            turn(todo[k], j, "x%d" % j)
+                        for j in range(2):
+                            gather(todo[k], j, "s")
+
+                def prep_done(k):
+                    if k < len(todo):
+                        prep_quantize(todo[k])
+
+                if i > 0:
+                    join_pairs(i - 1, 1)
+                stage1(i, 0)
+                scale_rows(i + 2, 0)
+                bias_planes(i, 0, [0, 1])
+                if i > 0:
+                    quantize(("y", i - 1, 1), "yq1")
+                prep(0)
+                scale_rows(i + 2, 1)
+                stage2(i - 1, [0, 1])
+                bias_planes(i, 0, [2, 3])
+                direct(i, 0)
+                scale_rows(i + 2, 2)
+                prep_done(0)
+                finish(i - 1, [0, 1])
+                store(i - 1, 0, 2)
+                scale_rows(i + 2, 3)
+                prep(1)
+                join_pairs(i, 0)
+                stage1(i, 1)
+                prep_done(1)
+                quantize(("y", i, 0), "yq0")
+                bias_planes(i, 1, [0, 1])
+                prep(2)
+                stage2(i - 1, [2, 3])
+                direct(i, 1)
+                finish(i - 1, [2, 3])
+                store(i - 1, 2, 2)
+                bias_planes(i, 1, [2, 3])
+                prep_done(2)
+
+            last = SLOTS - 1
+            join_pairs(last, 1)
+            quantize(("y", last, 1), "yq1")
+            for r in range(4):
+                stage2(last, [r])
+                finish(last, [r])
+                store(last, r, 1)

@@ -26,8 +26,8 @@ def tile_dummytemodel_pa_t_kernel(tc, hf_bytes, hf_scale, g1_w, g1_b, g2_w, g2_b
         const = ctx.enter_context(tc.tile_pool(name="const", bufs=1))
         raw = ctx.enter_context(tc.tile_pool(name="raw", bufs=1))
         work = ctx.enter_context(tc.tile_pool(name="work", bufs=3))
-        codes_pool = ctx.enter_context(tc.tile_pool(name="codes", bufs=2))
-        psum = ctx.enter_context(tc.psum_pool(name="psum", bufs=1))
+        codes_pool = ctx.enter_context(tc.tile_pool(name="codes", bufs=3))
+        psum = ctx.enter_context(tc.psum_pool(name="psum", bufs=8))
 
         ident = const.tile([P, P], F32)
         make_identity(nc, ident[:])
@@ -38,6 +38,7 @@ def tile_dummytemodel_pa_t_kernel(tc, hf_bytes, hf_scale, g1_w, g1_b, g2_w, g2_b
         hf_view = hf_bytes.rearrange("(g p r) k -> g p r k", g=G, r=8)
         out_view = out.rearrange("(g p r) n -> g p r n", g=G, r=8)
         scale = const.tile([P, 512], F32)
+        scale_t = const.tile([P, 4], F32)
         bias1_raw = const.tile([P, 8, 4], BF16)
         bias1 = const.tile([P, 8, 4], F32)
         bias2 = const.tile([P, G, 512], BF16)
@@ -60,28 +61,27 @@ def tile_dummytemodel_pa_t_kernel(tc, hf_bytes, hf_scale, g1_w, g1_b, g2_w, g2_b
         def load_w2(g):
             nc.sync.dma_start(out=w2raw[g][:], in_=g2_w[g].rearrange("(j p) k -> p j k", j=4))
 
-        nc.sync.dma_start(out=scale[:], in_=hf_scale.rearrange("o k -> (o k)").partition_broadcast(P))
+        nc.sync.dma_start(out=scale_t[:], in_=hf_scale.rearrange("o (m n) -> n (o m)", n=P))
         nc.sync.dma_start(out=hfb[0][:, 0:4, :], in_=hf_view[0][:, 0:4, :])
         load_w1(0, 0)
         load_w1(0, 1)
-        nc.sync.dma_start(out=bias1_raw[:], in_=g1_b.rearrange("g (h m t) -> m (g h) t", h=2, t=4))
         nc.sync.dma_start(out=hfb[0][:, 4:8, :], in_=hf_view[0][:, 4:8, :])
+        nc.sync.dma_start(out=bias1_raw[:], in_=g1_b.rearrange("g (h m t) -> m (g h) t", h=2, t=4))
         load_w2(0)
-        nc.sync.dma_start(
-            out=bias2[:].rearrange("p g n -> p (g n)"),
-            in_=g2_b.rearrange("g n -> (g n)").partition_broadcast(P),
-        )
         for g in range(1, G):
-            nc.sync.dma_start(out=hfb[g][:], in_=hf_view[g])
             load_w1(g, 0)
+            nc.sync.dma_start(out=hfb[g][:], in_=hf_view[g])
             load_w1(g, 1)
+            if g == 1:
+                nc.sync.dma_start(
+                    out=bias2[:].rearrange("p g n -> p (g n)"),
+                    in_=g2_b.rearrange("g n -> (g n)").partition_broadcast(P),
+                )
             load_w2(g)
 
         scaled = {}
 
         def scale_rows(i, r):
-            if i >= SLOTS:
-                return
             if r == 0:
                 hb = work.tile([P, 4, 512], BF16, tag="hb")
                 scaled[i] = hb
@@ -103,8 +103,8 @@ def tile_dummytemodel_pa_t_kernel(tc, hf_bytes, hf_scale, g1_w, g1_b, g2_w, g2_b
                 return w1raw[2 * a + b][:, row, :].bitcast(F32)
             return w2raw[a][:, row, 512 * b : 512 * (b + 1)].bitcast(F32)
 
-        def turn(unit, j, bank):
-            x = psum.tile([P, 512], F32, tag=bank)
+        def turn(unit, j):
+            x = psum.tile([P, 512], F32, tag="bank")
             xt[unit, j] = x
             view = x[:].rearrange("p (a u c) -> p a u c", a=2, u=2)
             for a in range(2):
@@ -150,8 +150,8 @@ def tile_dummytemodel_pa_t_kernel(tc, hf_bytes, hf_scale, g1_w, g1_b, g2_w, g2_b
 
         def mode(i, h):
             if i == SLOTS - 1:
-                return "direct" if h == 0 else "pairs"
-            return "half" if i % 2 == 0 and h == 1 else "pairs"
+                return "half" if h == 1 else "pairs"
+            return "half" if i % 2 == 0 and h == 0 else "pairs"
 
         first = {}
         pairs = {}
@@ -159,7 +159,7 @@ def tile_dummytemodel_pa_t_kernel(tc, hf_bytes, hf_scale, g1_w, g1_b, g2_w, g2_b
         def stage1(i, h):
             m = mode(i, h)
             for b in range(4):
-                bank = psum.tile([P, 512], F32, tag="c%d" % b)
+                bank = psum.tile([P, 512], F32, tag="bank")
                 first[i, h, b] = bank
                 if m == "pairs":
                     mx(bank[:], ("w1", i // 2, h), slice(128 * b, 128 * (b + 1)), ("hf", i, 0), slice(0, 512), True, True)
@@ -225,7 +225,7 @@ def tile_dummytemodel_pa_t_kernel(tc, hf_bytes, hf_scale, g1_w, g1_b, g2_w, g2_b
             if i < 0:
                 return
             for r in rs:
-                bank = psum.tile([P, 512], F32, tag="d%d" % (r % 2))
+                bank = psum.tile([P, 512], F32, tag="bank")
                 second[i, r] = bank
                 for h in range(2):
                     mx(bank[:], ("y", i, h), slice(128 * r, 128 * (r + 1)), ("w2", i // 2, h), slice(0, 512), h == 0, h == 1)
@@ -247,7 +247,7 @@ def tile_dummytemodel_pa_t_kernel(tc, hf_bytes, hf_scale, g1_w, g1_b, g2_w, g2_b
 
         def preps(i):
             g = i // 2
-            if i == SLOTS - 1:
+            if not -1 <= i < SLOTS - 1:
                 return []
             if i % 2 == 0:
                 return [("hf", i + 1, 0), ("w2", g, 0), ("w2", g, 1)]
@@ -255,80 +255,72 @@ def tile_dummytemodel_pa_t_kernel(tc, hf_bytes, hf_scale, g1_w, g1_b, g2_w, g2_b
 
         with tc.manual_schedule():
             nc.scalar.activation(out=warm_out[:], in_=warm[:], func=IDENTITY)
-            h0, a0, a1 = ("hf", 0, 0), ("w1", 0, 0), ("w1", 0, 1)
-            scale_rows(0, 0)
-            scale_rows(0, 1)
-            turn(h0, 0, "x0")
-            gather(h0, 0, "s")
-            scale_rows(0, 2)
-            scale_rows(0, 3)
-            turn(a0, 0, "c0")
-            turn(h0, 1, "x1")
-            turn(a0, 1, "c1")
-            gather(a0, 0, "s")
-            gather(h0, 1, "s")
-            gather(a0, 1, "v")
-            nc.vector.tensor_copy(out=bias1[:], in_=bias1_raw[:])
-            prep_quantize(h0)
-            prep_quantize(a0)
-            turn(a1, 0, "c2")
-            turn(a1, 1, "c3")
-            gather(a1, 0, "s")
-            gather(a1, 1, "v")
-            scale_rows(1, 0)
-            prep_quantize(a1)
-            for r in range(1, 4):
-                scale_rows(1, r)
+            spread = psum.tile([P, 512], F32, tag="bank")
+            for m in range(4):
+                nc.tensor.transpose(spread[:, 128 * m : 128 * (m + 1)], scale_t[:, m : m + 1].to_broadcast([P, P]), ident[:])
+            nc.scalar.copy(out=scale[:], in_=spread[:])
 
-            for i in range(SLOTS):
-                todo = preps(i)
+            def inside(i):
+                return 0 <= i < SLOTS
 
-                def prep(k):
-                    if k < len(todo):
-                        for j in range(2):
-                            turn(todo[k], j, "x%d" % j)
-                        for j in range(2):
-                            gather(todo[k], j, "s")
+            def turns(i, which):
+                for k, j in which:
+                    if preps(i):
+                        turn(preps(i)[k], j)
 
-                def prep_done(k):
-                    if k < len(todo):
-                        prep_quantize(todo[k])
+            def gathers(i, k, j, engine):
+                if preps(i):
+                    gather(preps(i)[k], j, engine)
 
-                if i > 0:
-                    join_pairs(i - 1, 1)
-                stage1(i, 0)
-                scale_rows(i + 2, 0)
-                bias_planes(i, 0, [0, 1])
-                if i > 0:
-                    quantize(("y", i - 1, 1), "yq1")
-                prep(0)
-                scale_rows(i + 2, 1)
-                stage2(i - 1, [0, 1])
-                bias_planes(i, 0, [2, 3])
-                direct(i, 0)
-                scale_rows(i + 2, 2)
-                prep_done(0)
-                finish(i - 1, [0, 1])
-                store(i - 1, 0, 2)
-                scale_rows(i + 2, 3)
-                prep(1)
-                join_pairs(i, 0)
-                stage1(i, 1)
-                prep_done(1)
-                quantize(("y", i, 0), "yq0")
-                bias_planes(i, 1, [0, 1])
-                prep(2)
-                stage2(i - 1, [2, 3])
-                direct(i, 1)
-                finish(i - 1, [2, 3])
-                store(i - 1, 2, 2)
-                bias_planes(i, 1, [2, 3])
-                prep_done(2)
+            def prep_q(i, k):
+                if preps(i):
+                    prep_quantize(preps(i)[k])
 
-            last = SLOTS - 1
-            join_pairs(last, 1)
-            quantize(("y", last, 1), "yq1")
-            for r in range(4):
-                stage2(last, [r])
-                finish(last, [r])
-                store(last, r, 1)
+            def rows(i, r0):
+                if inside(i):
+                    scale_rows(i, r0)
+                    scale_rows(i, r0 + 1)
+
+            def at(f, i, *args):
+                if inside(i):
+                    f(i, *args)
+
+            def y_quantize(i, h):
+                quantize(("y", i, h), "yq%d" % h)
+
+            def finish_store(i, r0):
+                finish(i, [r0, r0 + 1])
+                store(i, r0, 2)
+
+            for i in range(-2, SLOTS + 2):
+                prep_q(i - 1, 2)
+                rows(i + 2, 0)
+                at(direct, i, 0)
+                at(stage1, i, 1)
+                at(join_pairs, i - 1, 1)
+                rows(i + 2, 2)
+                at(y_quantize, i - 1, 0)
+                gathers(i, 0, 0, "s")
+                at(y_quantize, i - 1, 1)
+                gathers(i, 0, 1, "s")
+                at(stage2, i - 2, [2, 3])
+                at(stage2, i - 1, [0, 1])
+                prep_q(i, 0)
+                gathers(i, 1, 0, "s")
+                at(bias_planes, i, 0, [0, 1])
+                gathers(i, 1, 1, "s")
+                if i == -1:
+                    nc.vector.tensor_copy(out=bias1[:], in_=bias1_raw[:])
+                prep_q(i, 1)
+                turns(i + 1, [(0, 0), (0, 1), (1, 0)])
+                at(direct, i, 1)
+                gathers(i, 2, 0, "v")
+                at(bias_planes, i, 0, [2, 3])
+                at(finish_store, i - 2, 2)
+                at(finish_store, i - 1, 0)
+                gathers(i, 2, 1, "s")
+                at(stage1, i + 1, 0)
+                at(bias_planes, i, 1, [0, 1])
+                at(bias_planes, i, 1, [2, 3])
+                at(join_pairs, i, 0)
+                turns(i + 1, [(1, 1), (2, 0), (2, 1)])

@@ -37,10 +37,9 @@ def tile_dummytemodel_pa_t_kernel(tc, hf_bytes, hf_scale, g1_w, g1_b, g2_w, g2_b
 
         hf_view = hf_bytes.rearrange("(g p r) k -> g p r k", g=G, r=8)
         out_view = out.rearrange("(g p r) n -> g p r n", g=G, r=8)
-        scale = const.tile([P, 512], F32)
+        scale = const.tile([P, 1024], F32)
         scale_t = const.tile([P, 4], F32)
-        bias1_raw = const.tile([P, 8, 4], BF16)
-        bias1 = const.tile([P, 8, 4], F32)
+        bias1 = const.tile([P, 8, 4], BF16)
         bias2 = const.tile([P, G, 512], BF16)
         hfb, w1raw, w2raw = [], [], []
         for g in range(G):
@@ -66,7 +65,7 @@ def tile_dummytemodel_pa_t_kernel(tc, hf_bytes, hf_scale, g1_w, g1_b, g2_w, g2_b
         load_w1(0, 0)
         load_w1(0, 1)
         nc.sync.dma_start(out=hfb[0][:, 4:8, :], in_=hf_view[0][:, 4:8, :])
-        nc.sync.dma_start(out=bias1_raw[:], in_=g1_b.rearrange("g (h m t) -> m (g h) t", h=2, t=4))
+        nc.sync.dma_start(out=bias1[:], in_=g1_b.rearrange("g (h m t) -> m (g h) t", h=2, t=4))
         load_w2(0)
         for g in range(1, G):
             load_w1(g, 0)
@@ -85,12 +84,15 @@ def tile_dummytemodel_pa_t_kernel(tc, hf_bytes, hf_scale, g1_w, g1_b, g2_w, g2_b
             if r == 0:
                 hb = work.tile([P, 4, 512], BF16, tag="hb")
                 scaled[i] = hb
-            nc.vector.tensor_tensor(
-                out=scaled[i][:, r, :],
-                in0=hfb[i // 2][:, 4 * (i % 2) + r, :].bitcast(FP8),
-                in1=scale[:],
-                op=MULT,
-            )
+            n = 1 if i == 0 else 2
+            for r1 in range(r, r + 2, n):
+                row = 4 * (i % 2) + r1
+                nc.vector.tensor_tensor(
+                    out=scaled[i][:, r1 : r1 + n, :].rearrange("p r k -> p (r k)"),
+                    in0=hfb[i // 2][:, row : row + n, :].rearrange("p r k -> p (r k)").bitcast(FP8),
+                    in1=scale[:, 0 : 512 * n],
+                    op=MULT,
+                )
 
         grouped = {}
         xt = {}
@@ -149,9 +151,7 @@ def tile_dummytemodel_pa_t_kernel(tc, hf_bytes, hf_scale, g1_w, g1_b, g2_w, g2_b
             )
 
         def mode(i, h):
-            if i == SLOTS - 1:
-                return "half" if h == 1 else "pairs"
-            return "half" if i % 2 == 0 and h == 0 else "pairs"
+            return "half" if h == 0 else "pairs"
 
         first = {}
         pairs = {}
@@ -258,7 +258,8 @@ def tile_dummytemodel_pa_t_kernel(tc, hf_bytes, hf_scale, g1_w, g1_b, g2_w, g2_b
             spread = psum.tile([P, 512], F32, tag="bank")
             for m in range(4):
                 nc.tensor.transpose(spread[:, 128 * m : 128 * (m + 1)], scale_t[:, m : m + 1].to_broadcast([P, P]), ident[:])
-            nc.scalar.copy(out=scale[:], in_=spread[:])
+            for m in range(2):
+                nc.scalar.copy(out=scale[:, 512 * m : 512 * (m + 1)], in_=spread[:])
 
             def inside(i):
                 return 0 <= i < SLOTS
@@ -279,7 +280,6 @@ def tile_dummytemodel_pa_t_kernel(tc, hf_bytes, hf_scale, g1_w, g1_b, g2_w, g2_b
             def rows(i, r0):
                 if inside(i):
                     scale_rows(i, r0)
-                    scale_rows(i, r0 + 1)
 
             def at(f, i, *args):
                 if inside(i):
@@ -289,38 +289,40 @@ def tile_dummytemodel_pa_t_kernel(tc, hf_bytes, hf_scale, g1_w, g1_b, g2_w, g2_b
                 quantize(("y", i, h), "yq%d" % h)
 
             def finish_store(i, r0):
-                finish(i, [r0, r0 + 1])
-                store(i, r0, 2)
+                if i == SLOTS - 1:
+                    for r in (r0, r0 + 1):
+                        finish(i, [r])
+                        store(i, r, 1)
+                else:
+                    finish(i, [r0, r0 + 1])
+                    store(i, r0, 2)
 
-            for i in range(-2, SLOTS + 2):
-                prep_q(i - 1, 2)
-                rows(i + 2, 0)
-                at(direct, i, 0)
-                at(stage1, i, 1)
-                at(join_pairs, i - 1, 1)
+            for i in range(-3, SLOTS + 2):
                 rows(i + 2, 2)
-                at(y_quantize, i - 1, 0)
-                gathers(i, 0, 0, "s")
-                at(y_quantize, i - 1, 1)
-                gathers(i, 0, 1, "s")
-                at(stage2, i - 2, [2, 3])
-                at(stage2, i - 1, [0, 1])
-                prep_q(i, 0)
                 gathers(i, 1, 0, "s")
+                prep_q(i - 1, 2)
+                prep_q(i, 0)
+                at(stage1, i, 1)
                 at(bias_planes, i, 0, [0, 1])
-                gathers(i, 1, 1, "s")
-                if i == -1:
-                    nc.vector.tensor_copy(out=bias1[:], in_=bias1_raw[:])
-                prep_q(i, 1)
-                turns(i + 1, [(0, 0), (0, 1), (1, 0)])
-                at(direct, i, 1)
-                gathers(i, 2, 0, "v")
+                at(direct, i, 0)
                 at(bias_planes, i, 0, [2, 3])
-                at(finish_store, i - 2, 2)
-                at(finish_store, i - 1, 0)
+                at(join_pairs, i - 1, 1)
+                at(stage2, i - 2, [2, 3])
+                turns(i + 1, [(0, 0), (0, 1), (1, 0)])
+                gathers(i, 1, 1, "s")
+                gathers(i, 2, 0, "s")
                 gathers(i, 2, 1, "s")
-                at(stage1, i + 1, 0)
+                at(finish_store, i - 2, 0)
+                at(y_quantize, i - 1, 1)
                 at(bias_planes, i, 1, [0, 1])
-                at(bias_planes, i, 1, [2, 3])
                 at(join_pairs, i, 0)
+                at(stage2, i - 1, [0, 1])
+                at(finish_store, i - 2, 2)
+                prep_q(i, 1)
+                rows(i + 3, 0)
+                at(stage1, i + 1, 0)
                 turns(i + 1, [(1, 1), (2, 0), (2, 1)])
+                gathers(i + 1, 0, 0, "s")
+                gathers(i + 1, 0, 1, "s")
+                at(y_quantize, i, 0)
+                at(bias_planes, i, 1, [2, 3])

@@ -60,17 +60,18 @@ def tile_dummytemodel_pa_t_kernel(tc, hf_bytes, hf_scale, g1_w, g1_b, g2_w, g2_b
         def load_w2(g):
             nc.sync.dma_start(out=w2raw[g][:], in_=g2_w[g].rearrange("(j p) k -> p j k", j=4))
 
-        nc.sync.dma_start(out=scale_t[:], in_=hf_scale.rearrange("o (m n) -> n (o m)", n=P))
+        nc.sync.dma_start(out=scale_t[:], in_=hf_scale.rearrange("o (n t) -> n (o t)", t=4))
         nc.sync.dma_start(out=hfb[0][:, 0:4, :], in_=hf_view[0][:, 0:4, :])
         load_w1(0, 0)
         load_w1(0, 1)
         nc.sync.dma_start(out=hfb[0][:, 4:8, :], in_=hf_view[0][:, 4:8, :])
         nc.sync.dma_start(out=bias1[:], in_=g1_b.rearrange("g (h m t) -> m (g h) t", h=2, t=4))
-        load_w2(0)
-        for g in range(1, G):
-            load_w1(g, 0)
-            nc.sync.dma_start(out=hfb[g][:], in_=hf_view[g])
-            load_w1(g, 1)
+        for g in range(G):
+            if g > 0:
+                load_w1(g, 0)
+                load_w1(g, 1)
+            if g < G - 1:
+                nc.sync.dma_start(out=hfb[g + 1][:], in_=hf_view[g + 1])
             if g == 1:
                 nc.sync.dma_start(
                     out=bias2[:].rearrange("p g n -> p (g n)"),
@@ -151,7 +152,9 @@ def tile_dummytemodel_pa_t_kernel(tc, hf_bytes, hf_scale, g1_w, g1_b, g2_w, g2_b
             )
 
         def mode(i, h):
-            return "half" if h == 0 else "pairs"
+            if h == 0 and i < 2:
+                return "direct"
+            return "half" if h == 0 and i < SLOTS - 1 else "pairs"
 
         first = {}
         pairs = {}
@@ -230,14 +233,24 @@ def tile_dummytemodel_pa_t_kernel(tc, hf_bytes, hf_scale, g1_w, g1_b, g2_w, g2_b
                 for h in range(2):
                     mx(bank[:], ("y", i, h), slice(128 * r, 128 * (r + 1)), ("w2", i // 2, h), slice(0, 512), h == 0, h == 1)
 
-        def finish(i, rs):
-            if i < 0:
-                return
+        def finish(i, rs, parts=0):
             if rs[0] == 0:
                 o = work.tile([P, 4, 512], F32, tag="o")
                 results[i] = o
             for r in rs:
-                nc.vector.tensor_tensor(out=results[i][:, r, :], in0=second[i, r][:], in1=bias2[:, i // 2, :], op=ADD)
+                n = 512 // max(parts, 1)
+                for c in range(0, 512, n):
+                    nc.vector.tensor_tensor(
+                        out=results[i][:, r, c : c + n],
+                        in0=second[i, r][:, c : c + n],
+                        in1=bias2[:, i // 2, c : c + n],
+                        op=ADD,
+                    )
+                    if parts:
+                        nc.sync.dma_start(
+                            out=out_view[i // 2][:, 4 * (i % 2) + r, c : c + n],
+                            in_=results[i][:, r, c : c + n],
+                        )
 
         def store(i, r0, n):
             if i < 0:
@@ -259,7 +272,10 @@ def tile_dummytemodel_pa_t_kernel(tc, hf_bytes, hf_scale, g1_w, g1_b, g2_w, g2_b
             for m in range(4):
                 nc.tensor.transpose(spread[:, 128 * m : 128 * (m + 1)], scale_t[:, m : m + 1].to_broadcast([P, P]), ident[:])
             for m in range(2):
-                nc.scalar.copy(out=scale[:, 512 * m : 512 * (m + 1)], in_=spread[:])
+                nc.scalar.copy(
+                    out=scale[:, 512 * m : 512 * (m + 1)].rearrange("p (n t) -> p n t", t=4),
+                    in_=spread[:].rearrange("p (t n) -> p n t", t=4),
+                )
 
             def inside(i):
                 return 0 <= i < SLOTS
@@ -291,38 +307,37 @@ def tile_dummytemodel_pa_t_kernel(tc, hf_bytes, hf_scale, g1_w, g1_b, g2_w, g2_b
             def finish_store(i, r0):
                 if i == SLOTS - 1:
                     for r in (r0, r0 + 1):
-                        finish(i, [r])
-                        store(i, r, 1)
+                        finish(i, [r], 2 if r == 3 else 1)
                 else:
                     finish(i, [r0, r0 + 1])
                     store(i, r0, 2)
 
             for i in range(-3, SLOTS + 2):
                 rows(i + 2, 2)
-                gathers(i, 1, 0, "s")
                 prep_q(i - 1, 2)
-                prep_q(i, 0)
+                gathers(i, 1, 0, "s")
                 at(stage1, i, 1)
                 at(bias_planes, i, 0, [0, 1])
-                at(direct, i, 0)
                 at(bias_planes, i, 0, [2, 3])
+                prep_q(i, 0)
+                gathers(i, 1, 1, "s")
+                turns(i + 1, [(0, 0), (0, 1), (1, 0)])
+                at(direct, i, 0)
+                at(finish_store, i - 2, 0)
+                gathers(i, 2, 0, "s")
                 at(join_pairs, i - 1, 1)
                 at(stage2, i - 2, [2, 3])
-                turns(i + 1, [(0, 0), (0, 1), (1, 0)])
-                gathers(i, 1, 1, "s")
-                gathers(i, 2, 0, "s")
                 gathers(i, 2, 1, "s")
-                at(finish_store, i - 2, 0)
-                at(y_quantize, i - 1, 1)
-                at(bias_planes, i, 1, [0, 1])
-                at(join_pairs, i, 0)
-                at(stage2, i - 1, [0, 1])
-                at(finish_store, i - 2, 2)
                 prep_q(i, 1)
-                rows(i + 3, 0)
-                at(stage1, i + 1, 0)
-                turns(i + 1, [(1, 1), (2, 0), (2, 1)])
+                at(bias_planes, i, 1, [0, 1])
                 gathers(i + 1, 0, 0, "s")
+                at(stage1, i + 1, 0)
+                rows(i + 3, 0)
+                turns(i + 1, [(1, 1), (2, 0), (2, 1)])
+                at(y_quantize, i - 1, 1)
+                at(stage2, i - 1, [0, 1])
                 gathers(i + 1, 0, 1, "s")
-                at(y_quantize, i, 0)
+                at(join_pairs, i, 0)
+                at(finish_store, i - 2, 2)
                 at(bias_planes, i, 1, [2, 3])
+                at(y_quantize, i, 0)

from contextlib import ExitStack

import concourse.mybir as mybir
from concourse.masks import make_identity

F32 = mybir.dt.float32
BF16 = mybir.dt.bfloat16
U32 = mybir.dt.uint32
U8 = mybir.dt.uint8
FP8 = mybir.dt.float8_e4m3fn
FP8X4 = mybir.dt.float8_e4m3fn_x4
ADD = mybir.AluOpType.add
MULT = mybir.AluOpType.mult
IDENTITY = mybir.ActivationFunctionType.Identity

FLOPS = 2 * 4096 * 512 * 1024 * 2

P = 128
G = 4
SLOTS = 8


def tile_dummytemodel_pa_t_kernel(tc, hf_bytes, hf_scale, g1_w, g1_b, g2_w, g2_b, out):
    nc = tc.nc
    with ExitStack() as ctx:
        const = ctx.enter_context(tc.tile_pool(name="const", bufs=1))
        raw = ctx.enter_context(tc.tile_pool(name="raw", bufs=1))
        work = ctx.enter_context(tc.tile_pool(name="work", bufs=3))
        codes_pool = ctx.enter_context(tc.tile_pool(name="codes", bufs=3))
        psum = ctx.enter_context(tc.psum_pool(name="psum", bufs=8))

        ident = const.tile([P, P], F32)
        make_identity(nc, ident[:])
        warm = const.tile([P, 1], F32)
        warm_out = const.tile([P, 1], F32)
        nc.gpsimd.memset(warm[:], 0.0)

        hf_view = hf_bytes.rearrange("(g p r) k -> g p r k", g=G, r=8)
        out_view = out.rearrange("(g p r) n -> g p r n", g=G, r=8)
        scale = const.tile([P, 1024], F32)
        scale_t = const.tile([P, 4], F32)
        bias1 = const.tile([P, 8, 4], BF16)
        bias2 = const.tile([P, G, 512], BF16)
        hfb, w1raw, w2raw = [], [], []
        for g in range(G):
            hf_tile = raw.tile([P, 8, 512], U8, tag="hfb%d" % g)
            hfb.append(hf_tile)
            for h in range(2):
                w1_tile = raw.tile([P, 4, 512], BF16, tag="w1_%d_%d" % (g, h))
                w1raw.append(w1_tile)
            w2_tile = raw.tile([P, 4, 1024], BF16, tag="w2_%d" % g)
            w2raw.append(w2_tile)

        def load_w1(g, h):
            nc.sync.dma_start(
                out=w1raw[2 * g + h][:],
                in_=g1_w[g].rearrange("(h m t) k -> h m t k", h=2, t=4)[h],
            )

        def load_w2(g):
            nc.sync.dma_start(out=w2raw[g][:], in_=g2_w[g].rearrange("(j p) k -> p j k", j=4))

        nc.sync.dma_start(out=scale_t[:], in_=hf_scale.rearrange("o (n t) -> n (o t)", t=4))
        nc.sync.dma_start(out=hfb[0][:, 0:4, :], in_=hf_view[0][:, 0:4, :])
        load_w1(0, 0)
        load_w1(0, 1)
        nc.sync.dma_start(out=hfb[0][:, 4:8, :], in_=hf_view[0][:, 4:8, :])
        nc.sync.dma_start(out=bias1[:], in_=g1_b.rearrange("g (h m t) -> m (g h) t", h=2, t=4))
        for g in range(G):
            if g > 0:
                load_w1(g, 0)
                load_w1(g, 1)
            if g < G - 1:
                nc.sync.dma_start(out=hfb[g + 1][:], in_=hf_view[g + 1])
            if g == 1:
                nc.sync.dma_start(
                    out=bias2[:].rearrange("p g n -> p (g n)"),
                    in_=g2_b.rearrange("g n -> (g n)").partition_broadcast(P),
                )
            load_w2(g)

        scaled = {}

        def scale_rows(i, r):
            if r == 0:
                hb = work.tile([P, 4, 512], BF16, tag="hb")
                scaled[i] = hb
            n = 1 if i == 0 else 2
            for r1 in range(r, r + 2, n):
                row = 4 * (i % 2) + r1
                nc.vector.tensor_tensor(
                    out=scaled[i][:, r1 : r1 + n, :].rearrange("p r k -> p (r k)"),
                    in0=hfb[i // 2][:, row : row + n, :].rearrange("p r k -> p (r k)").bitcast(FP8),
                    in1=scale[:, 0 : 512 * n],
                    op=MULT,
                )

        grouped = {}
        xt = {}

        def words(unit, row):
            kind, a, b = unit
            if kind == "hf":
                return scaled[a][:, row, :].bitcast(F32)
            if kind == "w1":
                return w1raw[2 * a + b][:, row, :].bitcast(F32)
            return w2raw[a][:, row, 512 * b : 512 * (b + 1)].bitcast(F32)

        def turn(unit, j):
            x = psum.tile([P, 512], F32, tag="bank")
            xt[unit, j] = x
            view = x[:].rearrange("p (a u c) -> p a u c", a=2, u=2)
            for a in range(2):
                w = words(unit, 2 * j + a)
                for u in range(2):
                    nc.tensor.transpose(view[:, a, u, :], w[:, u:256:2], ident[:])

        def gather(unit, j, engine):
            if j == 0:
                grp = work.tile([P, 2048], BF16, tag="grp", align_bytes=64)
                grouped[unit] = grp
            dst = grouped[unit][:].bitcast(F32)[:, 512 * j : 512 * (j + 1)].rearrange("p (a c u) -> p a c u", a=2, u=2)
            srcv = xt[unit, j][:].rearrange("p (a u c) -> p a c u", a=2, u=2)
            if engine == "s":
                nc.scalar.copy(out=dst, in_=srcv)
            else:
                nc.vector.tensor_copy(out=dst, in_=srcv)

        codes = {}

        def quantize(unit, tag):
            q = codes_pool.tile([P, 512], U32, tag=tag, align_bytes=64)
            s = codes_pool.tile([P, 512], U8, tag=tag + "s", align_bytes=64)
            codes[unit] = (q, s)
            nc.vector.quantize_mx(out=q[:].bitcast(FP8X4), scales=s[:], in_=grouped[unit][:])

        def prep_quantize(unit):
            kind, a, b = unit
            quantize(unit, "hfq" if kind == "hf" else "%sq%d" % (kind, b))

        def mx(dst, left, lcols, right, rcols, start, stop):
            lq, ls = codes[left]
            rq, rs = codes[right]
            nc.tensor.matmul_mx(
                out=dst,
                lhsT=lq[:, lcols].bitcast(FP8X4),
                lhsT_scale=ls[:, lcols],
                rhs=rq[:, rcols].bitcast(FP8X4),
                rhs_scale=rs[:, rcols],
                start=start,
                stop=stop,
            )

        def mode(i, h):
            if h == 0 and i < 2:
                return "direct"
            return "half" if h == 0 and i < SLOTS - 1 else "pairs"

        first = {}
        pairs = {}

        def stage1(i, h):
            m = mode(i, h)
            for b in range(4):
                bank = psum.tile([P, 512], F32, tag="bank")
                first[i, h, b] = bank
                if m == "pairs":
                    mx(bank[:], ("w1", i // 2, h), slice(128 * b, 128 * (b + 1)), ("hf", i, 0), slice(0, 512), True, True)
                elif m == "half" and b < 2:
                    for e in range(2):
                        t = 2 * b + e
                        mx(bank[:, 256 * e : 256 * (e + 1)], ("w1", i // 2, h), slice(128 * t, 128 * (t + 1)), ("hf", i, 0), slice(0, 256), True, True)
                else:
                    for t in range(4):
                        mx(bank[:, 128 * t : 128 * (t + 1)], ("w1", i // 2, h), slice(128 * t, 128 * (t + 1)), ("hf", i, 0), slice(128 * b, 128 * (b + 1)), True, True)

        def bias_planes(i, h, ts):
            m = mode(i, h)
            if m == "direct":
                return
            n = 512 if m == "pairs" else 256
            if ts[0] == 0:
                y2 = work.tile([P, 2, 512, 2], BF16, tag="y2", align_bytes=64)
                pairs[i, h] = y2
            for t in ts:
                src = first[i, h, t][:] if m == "pairs" else first[i, h, t // 2][:, 256 * (t % 2) : 256 * (t % 2 + 1)]
                nc.scalar.activation(
                    out=pairs[i, h][:, t // 2, 0:n, t % 2],
                    in_=src,
                    func=IDENTITY,
                    bias=bias1[:, 2 * (i // 2) + h, t : t + 1],
                )

        def y_tile(i, h):
            if ("y", i, h) not in grouped:
                yg = work.tile([P, 2048], BF16, tag="yg", align_bytes=64)
                grouped["y", i, h] = yg
            return grouped["y", i, h]

        def join_pairs(i, h):
            m = mode(i, h)
            yg = y_tile(i, h)
            if m == "direct":
                return
            n = 512 if m == "pairs" else 256
            nc.vector.tensor_copy(
                out=yg[:].bitcast(F32)[:, 0 : 2 * n].rearrange("p (n u) -> p n u", u=2),
                in_=pairs[i, h][:].rearrange("p u n e -> p (u n e)").bitcast(F32).rearrange("p (u n) -> p n u", u=2)[:, 0:n, :],
            )

        def direct(i, h):
            m = mode(i, h)
            if m == "pairs":
                return
            yg = y_tile(i, h)
            for b in range(0 if m == "direct" else 2, 4):
                nc.vector.tensor_tensor(
                    out=yg[:, 512 * b : 512 * (b + 1)].rearrange("p (n t) -> p n t", t=4),
                    in0=first[i, h, b][:].rearrange("p (t n) -> p n t", t=4),
                    in1=bias1[:, 2 * (i // 2) + h : 2 * (i // 2) + h + 1, :].to_broadcast([P, 128, 4]),
                    op=ADD,
                )

        second = {}
        results = {}

        def stage2(i, rs):
            if i < 0:
                return
            for r in rs:
                bank = psum.tile([P, 512], F32, tag="bank")
                second[i, r] = bank
                for h in range(2):
                    mx(bank[:], ("y", i, h), slice(128 * r, 128 * (r + 1)), ("w2", i // 2, h), slice(0, 512), h == 0, h == 1)

        def finish(i, rs, parts=0):
            if rs[0] == 0:
                o = work.tile([P, 4, 512], F32, tag="o")
                results[i] = o
            for r in rs:
                n = 512 // max(parts, 1)
                for c in range(0, 512, n):
                    nc.vector.tensor_tensor(
                        out=results[i][:, r, c : c + n],
                        in0=second[i, r][:, c : c + n],
                        in1=bias2[:, i // 2, c : c + n],
                        op=ADD,
                    )
                    if parts:
                        nc.sync.dma_start(
                            out=out_view[i // 2][:, 4 * (i % 2) + r, c : c + n],
                            in_=results[i][:, r, c : c + n],
                        )

        def store(i, r0, n):
            if i < 0:
                return
            first_row = 4 * (i % 2) + r0
            nc.sync.dma_start(out=out_view[i // 2][:, first_row : first_row + n, :], in_=results[i][:, r0 : r0 + n, :])

        def preps(i):
            g = i // 2
            if not -1 <= i < SLOTS - 1:
                return []
            if i % 2 == 0:
                return [("hf", i + 1, 0), ("w2", g, 0), ("w2", g, 1)]
            return [("w1", g + 1, 0), ("hf", i + 1, 0), ("w1", g + 1, 1)]

        with tc.manual_schedule():
            nc.scalar.activation(out=warm_out[:], in_=warm[:], func=IDENTITY)
            spread = psum.tile([P, 512], F32, tag="bank")
            for m in range(4):
                nc.tensor.transpose(spread[:, 128 * m : 128 * (m + 1)], scale_t[:, m : m + 1].to_broadcast([P, P]), ident[:])
            for m in range(2):
                nc.scalar.copy(
                    out=scale[:, 512 * m : 512 * (m + 1)].rearrange("p (n t) -> p n t", t=4),
                    in_=spread[:].rearrange("p (t n) -> p n t", t=4),
                )

            def inside(i):
                return 0 <= i < SLOTS

            def turns(i, which):
                for k, j in which:
                    if preps(i):
                        turn(preps(i)[k], j)

            def gathers(i, k, j, engine):
                if preps(i):
                    gather(preps(i)[k], j, engine)

            def prep_q(i, k):
                if preps(i):
                    prep_quantize(preps(i)[k])

            def rows(i, r0):
                if inside(i):
                    scale_rows(i, r0)

            def at(f, i, *args):
                if inside(i):
                    f(i, *args)

            def y_quantize(i, h):
                quantize(("y", i, h), "yq%d" % h)

            def finish_store(i, r0):
                if i == SLOTS - 1:
                    for r in (r0, r0 + 1):
                        finish(i, [r], 2 if r == 3 else 1)
                else:
                    finish(i, [r0, r0 + 1])
                    store(i, r0, 2)

            for i in range(-3, SLOTS + 2):
                rows(i + 2, 2)
                prep_q(i - 1, 2)
                gathers(i, 1, 0, "s")
                at(stage1, i, 1)
                at(bias_planes, i, 0, [0, 1])
                at(bias_planes, i, 0, [2, 3])
                prep_q(i, 0)
                gathers(i, 1, 1, "s")
                turns(i + 1, [(0, 0), (0, 1), (1, 0)])
                at(direct, i, 0)
                at(finish_store, i - 2, 0)
                gathers(i, 2, 0, "s")
                at(join_pairs, i - 1, 1)
                at(stage2, i - 2, [2, 3])
                gathers(i, 2, 1, "s")
                prep_q(i, 1)
                at(bias_planes, i, 1, [0, 1])
                gathers(i + 1, 0, 0, "s")
                at(stage1, i + 1, 0)
                rows(i + 3, 0)
                turns(i + 1, [(1, 1), (2, 0), (2, 1)])
                at(y_quantize, i - 1, 1)
                at(stage2, i - 1, [0, 1])
                gathers(i + 1, 0, 1, "s")
                at(join_pairs, i, 0)
                at(finish_store, i - 2, 2)
                at(bias_planes, i, 1, [2, 3])
                at(y_quantize, i, 0)
